import numpy as np
import ml_dtypes


def mxq(x, axis, fmt="e4m3"):
    dtype, down = {"e4m3": (ml_dtypes.float8_e4m3fn, 7), "e5m2": (ml_dtypes.float8_e5m2, 14)}[fmt]
    v = np.moveaxis(np.asarray(x, np.float32).astype(ml_dtypes.bfloat16).astype(np.float64), axis, -1)
    blocks = v.reshape(v.shape[:-1] + (-1, 32))
    amax = np.abs(blocks).max(-1, keepdims=True)
    byte = np.maximum(np.where(amax > 0, np.frexp(amax)[1] - 1 + 127, 0) - down, 1)
    scale = np.exp2(byte - 127.0)
    codes = (blocks / scale).astype(np.float32).astype(dtype).astype(np.float64)
    return np.moveaxis((codes * scale).reshape(v.shape), -1, axis)


WIDE = False


def mx_kscale(k):
    if not WIDE:
        return np.ones(k)
    levels = np.array([10, -10, 5, -5, 0])
    if k % 512:
        return np.exp2(np.random.permutation(np.resize(levels, k // 32))).repeat(32)
    a = np.empty((k // 512, 16))
    for p in range(k // 512):
        a[p, :8] = np.random.permutation(np.resize(levels, 8))
        for g in range(8):
            far = levels[np.abs(levels - a[p, g]) >= 10]
            a[p, g + 8] = far[np.random.randint(len(far))]
    return np.exp2(a.ravel()).repeat(32)


BF16 = ml_dtypes.bfloat16


def bf(x):
    return np.asarray(x, np.float32).astype(BF16)


def f64(x):
    return np.asarray(x).astype(np.float64)


E2M1 = np.array([0.0, 0.5, 1.0, 1.5, 2.0, 3.0, 4.0, 6.0, -0.0, -0.5, -1.0, -1.5, -2.0, -3.0, -4.0, -6.0])


def pack_weight(w, fmt):
    k, n = w.shape
    w = f64(bf(w)).reshape(k // 32, 32, n)
    amax = np.abs(w).max(1)
    if fmt == "e4m3":
        byte = np.frexp(amax)[1] - 1 + 127 - 7
    else:
        mant, ex = np.frexp(amax / 6.0)
        byte = np.where(mant > 0.5, ex, ex - 1) + 127
    byte = np.clip(np.where(amax > 0, byte, 1), 1, 254)
    scaled = (w * np.exp2(127.0 - byte)[:, None, :]).reshape(k, n).astype(np.float32)
    by_word = np.ascontiguousarray(scaled.reshape(k // 512, 128, 4, n).transpose(0, 1, 3, 2))
    if fmt == "e4m3":
        words = by_word.astype(ml_dtypes.float8_e4m3fn).view(np.uint8)
    else:
        c = by_word.astype(ml_dtypes.float4_e2m1fn).view(np.uint8) & 0xF
        words = c[..., 0::2] | (c[..., 1::2] << 4)
    return np.ascontiguousarray(words), np.ascontiguousarray(byte.astype(np.uint8).reshape(k // 512, 16, n))


def unpack_weight(words, scales, fmt):
    g, p, n, _ = words.shape
    if fmt == "e4m3":
        vals = np.ascontiguousarray(words).view(ml_dtypes.float8_e4m3fn).astype(np.float64)
    else:
        nib = np.empty((g, p, n, 4), np.uint8)
        nib[..., 0::2] = words & 0xF
        nib[..., 1::2] = words >> 4
        vals = E2M1[nib]
    vals = vals * np.repeat(np.exp2(scales.astype(np.float64) - 127.0), 8, axis=1)[..., None]
    return vals.transpose(0, 1, 3, 2).reshape(g * 512, n)


B, S, D, NH, LAT, F = 4, 128, 2048, 16, 512, 8192
EPS = 1e-5


def layer_norm(c, g, b):
    m = c.mean(-1, keepdims=True)
    v = ((c - m) ** 2).mean(-1, keepdims=True)
    return (c - m) * (1.0 / np.sqrt(v + EPS)) * g + b


def down_weight():
    return (np.random.standard_normal((D, LAT)) + 0.3 * np.random.standard_normal((D, 1))) / np.sqrt(D)


def draw0():
    s = mx_kscale(D)
    tq, tkv = mx_kscale(LAT), mx_kscale(LAT)
    normed = bf(np.random.standard_normal((B, S, D)) * s)
    W_dq_words, W_dq_scales = pack_weight(down_weight() / s[:, None], "e4m3")
    q_ln_g = bf((1.0 + 0.1 * np.random.standard_normal(LAT)) * tq)
    q_ln_b = bf(0.1 * np.random.standard_normal(LAT) * tq)
    W_uq_words, W_uq_scales = pack_weight(np.random.standard_normal((LAT, D)) / np.sqrt(LAT) / tq[:, None], "e4m3")
    W_dkv_words, W_dkv_scales = pack_weight(down_weight() / s[:, None], "e4m3")
    kv_ln_g = bf((1.0 + 0.1 * np.random.standard_normal(LAT)) * tkv)
    kv_ln_b = bf(0.1 * np.random.standard_normal(LAT) * tkv)
    W_ukv_words, W_ukv_scales = pack_weight(np.random.standard_normal((LAT, D + D)) / np.sqrt(LAT) / tkv[:, None], "e4m3")
    return {
        "normed": normed,
        "W_dq_words": W_dq_words,
        "W_dq_scales": W_dq_scales,
        "q_ln_g": q_ln_g,
        "q_ln_b": q_ln_b,
        "W_uq_words": W_uq_words,
        "W_uq_scales": W_uq_scales,
        "W_dkv_words": W_dkv_words,
        "W_dkv_scales": W_dkv_scales,
        "kv_ln_g": kv_ln_g,
        "kv_ln_b": kv_ln_b,
        "W_ukv_words": W_ukv_words,
        "W_ukv_scales": W_ukv_scales,
    }


def core(normed, W_dq_words, W_dq_scales, q_ln_g, q_ln_b, W_uq_words, W_uq_scales, W_dkv_words, W_dkv_scales, kv_ln_g, kv_ln_b, W_ukv_words, W_ukv_scales):
    nq = mxq(f64(normed), 2, "e4m3")
    cq = layer_norm(nq @ unpack_weight(W_dq_words, W_dq_scales, "e4m3"), f64(q_ln_g), f64(q_ln_b))
    Q = mxq(cq, 2, "e4m3") @ unpack_weight(W_uq_words, W_uq_scales, "e4m3")
    ckv = layer_norm(nq @ unpack_weight(W_dkv_words, W_dkv_scales, "e4m3"), f64(kv_ln_g), f64(kv_ln_b))
    KV = mxq(ckv, 2, "e4m3") @ unpack_weight(W_ukv_words, W_ukv_scales, "e4m3")
    return Q, KV


def e4m3fn_bytes(y):
    return np.clip(np.asarray(y, np.float64), -448.0, 448.0).astype(np.float32).astype(ml_dtypes.float8_e4m3fn).view(np.uint8)


def e4m3fn_values(b):
    return np.asarray(b, np.uint8).view(ml_dtypes.float8_e4m3fn).astype(np.float64)


def setup_inputs():
    d = draw0()
    x0 = np.asarray(d['normed']).astype(np.float64)
    s = (np.max(np.abs(x0), axis=(0, 1), keepdims=True) / 448.0).astype(np.float32)
    out = {}
    for k, v in d.items():
        if k == 'normed':
            out['normed_bytes'] = e4m3fn_bytes(x0 / s.astype(np.float64))
            out['normed_scale'] = s
        else:
            out[k] = v
    return out


def reference(normed_bytes, normed_scale, W_dq_words, W_dq_scales, q_ln_g, q_ln_b, W_uq_words, W_uq_scales, W_dkv_words, W_dkv_scales, kv_ln_g, kv_ln_b, W_ukv_words, W_ukv_scales):
    return core(e4m3fn_values(normed_bytes) * normed_scale.astype(np.float64), W_dq_words, W_dq_scales, q_ln_g, q_ln_b, W_uq_words, W_uq_scales, W_dkv_words, W_dkv_scales, kv_ln_g, kv_ln_b, W_ukv_words, W_ukv_scales)

@@ -1,0 +1,477 @@
+from contextlib import ExitStack
+
+import concourse.mybir as mybir
+from concourse.masks import make_identity
+
+B, S, D, LAT = 4, 128, 2048, 512
+N_Q, N_KV = 2048, 4096
+EPS = 1e-5
+FLOPS = 2 * B * S * D * (LAT + LAT) + 2 * B * S * LAT * (N_Q + N_KV)
+
+P = 128
+PACK = 4
+K_PASS = 512
+PASSES = D // K_PASS
+BANK = 512
+
+F32 = mybir.dt.float32
+BF16 = mybir.dt.bfloat16
+U32 = mybir.dt.uint32
+U8 = mybir.dt.uint8
+I32 = mybir.dt.int32
+FP8 = mybir.dt.float8_e4m3fn
+FP8X4 = mybir.dt.float8_e4m3fn_x4
+ALU = mybir.AluOpType
+ACT = mybir.ActivationFunctionType
+NB, NL, NT = 4, 2, 2
+ORDER = [
+    ("widen", 0, 0),
+    ("widen", 0, 1),
+    ("widen", 0, 2),
+    ("turn", 0, 0),
+    ("widen", 0, 3),
+    ("lay", 0, 0),
+    ("widen", 1, 0),
+    ("turn", 0, 1),
+    ("qx", 0, 0),
+    ("widen", 1, 1),
+    ("lay", 0, 1),
+    ("widen", 2, 0),
+    ("amm", 2),
+    ("amm", 1),
+    ("qx", 0, 1),
+    ("acopy", 2),
+    ("widen", 2, 1),
+    ("project", 0, "kv"),
+    ("acopy", 1),
+    ("widen", 2, 2),
+    ("widen", 2, 3),
+    ("amm", 3),
+    ("project", 0, "q"),
+    ("stats", 0, "kv"),
+    ("acopy", 3),
+    ("widen", 1, 2),
+    ("amm", 0),
+    ("stats", 0, "q"),
+    ("turn", 2, 0),
+    ("acopy", 0),
+    ("agg", 0, "kv"),
+    ("widen", 1, 3),
+    ("lay", 2, 0),
+    ("pow", 0, "kv"),
+    ("turn", 2, 1),
+    ("center", 0, "kv"),
+    ("turn", 1, 0),
+    ("lay", 2, 1),
+    ("qx", 2, 0),
+    ("agg", 0, "q"),
+    ("lay", 1, 0),
+    ("finish", 0, "kv"),
+    ("turn", 1, 1),
+    ("pow", 0, "q"),
+    ("center", 0, "q"),
+    ("tl", 0, "kv"),
+    ("lay", 1, 1),
+    ("qx", 2, 1),
+    ("ll", 0, "kv"),
+    ("finish", 0, "q"),
+    ("project", 2, "kv"),
+    ("qx", 1, 0),
+    ("ql", 0, "kv"),
+    ("qx", 1, 1),
+    ("tl", 0, "q"),
+    ("widen", 3, 0),
+    ("mm", 0, "kv", 0),
+    ("ll", 0, "q"),
+    ("project", 1, "kv"),
+    ("stats", 2, "kv"),
+    ("drain", 0, "kv", 0, "S"),
+    ("ql", 0, "q"),
+    ("agg", 2, "kv"),
+    ("widen", 3, 1),
+    ("mm", 0, "kv", 1),
+    ("pow", 2, "kv"),
+    ("mm", 0, "q", 0),
+    ("drain", 0, "kv", 1, "S"),
+    ("stats", 1, "kv"),
+    ("mm", 0, "q", 1),
+    ("mm", 0, "q", 2),
+    ("drain", 0, "q", 0, "S"),
+    ("turn", 3, 0),
+    ("drain", 0, "q", 1, "V"),
+    ("drain", 0, "q", 2, "S"),
+    ("mm", 0, "q", 3),
+    ("agg", 1, "kv"),
+    ("center", 2, "kv"),
+    ("mm", 0, "kv", 2),
+    ("pow", 1, "kv"),
+    ("drain", 0, "q", 3, "S"),
+    ("mm", 0, "kv", 3),
+    ("center", 1, "kv"),
+    ("mm", 0, "kv", 4),
+    ("drain", 0, "kv", 2, "S"),
+    ("project", 1, "q"),
+    ("finish", 2, "kv"),
+    ("drain", 0, "kv", 3, "S"),
+    ("finish", 1, "kv"),
+    ("drain", 0, "kv", 4, "S"),
+    ("tl", 2, "kv"),
+    ("mm", 0, "kv", 5),
+    ("stats", 1, "q"),
+    ("ll", 2, "kv"),
+    ("mm", 0, "kv", 6),
+    ("mm", 0, "kv", 7),
+    ("drain", 0, "kv", 5, "S"),
+    ("widen", 3, 2),
+    ("project", 2, "q"),
+    ("drain", 0, "kv", 6, "S"),
+    ("agg", 1, "q"),
+    ("ql", 2, "kv"),
+    ("center", 1, "q"),
+    ("pow", 1, "q"),
+    ("lay", 3, 0),
+    ("mm", 2, "kv", 0),
+    ("widen", 3, 3),
+    ("mm", 2, "kv", 1),
+    ("drain", 0, "kv", 7, "S"),
+    ("tl", 1, "kv"),
+    ("drain", 2, "kv", 0, "V"),
+    ("mm", 2, "kv", 2),
+    ("drain", 2, "kv", 1, "S"),
+    ("mm", 2, "kv", 3),
+    ("finish", 1, "q"),
+    ("turn", 3, 1),
+    ("ll", 1, "kv"),
+    ("drain", 2, "kv", 2, "S"),
+    ("drain", 2, "kv", 3, "V"),
+    ("mm", 2, "kv", 4),
+    ("tl", 1, "q"),
+    ("lay", 3, 1),
+    ("ql", 1, "kv"),
+    ("mm", 2, "kv", 5),
+    ("drain", 2, "kv", 4, "V"),
+    ("mm", 2, "kv", 6),
+    ("ll", 1, "q"),
+    ("mm", 1, "kv", 0),
+    ("drain", 2, "kv", 5, "S"),
+    ("qx", 3, 0),
+    ("mm", 1, "kv", 1),
+    ("drain", 1, "kv", 0, "V"),
+    ("drain", 2, "kv", 6, "S"),
+    ("mm", 1, "kv", 2),
+    ("drain", 1, "kv", 1, "V"),
+    ("drain", 1, "kv", 2, "S"),
+    ("mm", 1, "kv", 3),
+    ("ql", 1, "q"),
+    ("mm", 1, "kv", 4),
+    ("qx", 3, 1),
+    ("drain", 1, "kv", 3, "S"),
+    ("mm", 1, "kv", 5),
+    ("stats", 2, "q"),
+    ("mm", 1, "q", 0),
+    ("drain", 1, "kv", 4, "S"),
+    ("project", 3, "q"),
+    ("drain", 1, "kv", 5, "V"),
+    ("drain", 1, "q", 0, "S"),
+    ("agg", 2, "q"),
+    ("center", 2, "q"),
+    ("pow", 2, "q"),
+    ("mm", 1, "kv", 6),
+    ("mm", 1, "q", 1),
+    ("drain", 1, "kv", 6, "S"),
+    ("stats", 3, "q"),
+    ("mm", 1, "kv", 7),
+    ("mm", 1, "q", 2),
+    ("drain", 1, "q", 1, "S"),
+    ("drain", 1, "kv", 7, "V"),
+    ("project", 3, "kv"),
+    ("drain", 1, "q", 2, "S"),
+    ("agg", 3, "q"),
+    ("finish", 2, "q"),
+    ("pow", 3, "q"),
+    ("mm", 1, "q", 3),
+    ("center", 3, "q"),
+    ("mm", 2, "kv", 7),
+    ("drain", 1, "q", 3, "S"),
+    ("tl", 2, "q"),
+    ("stats", 3, "kv"),
+    ("ll", 2, "q"),
+    ("finish", 3, "q"),
+    ("drain", 2, "kv", 7, "S"),
+    ("agg", 3, "kv"),
+    ("ql", 2, "q"),
+    ("tl", 3, "q"),
+    ("pow", 3, "kv"),
+    ("center", 3, "kv"),
+    ("mm", 2, "q", 0),
+    ("ll", 3, "q"),
+    ("mm", 2, "q", 1),
+    ("drain", 2, "q", 0, "V"),
+    ("mm", 2, "q", 2),
+    ("drain", 2, "q", 1, "S"),
+    ("mm", 2, "q", 3),
+    ("ql", 3, "q"),
+    ("drain", 2, "q", 2, "V"),
+    ("drain", 2, "q", 3, "S"),
+    ("mm", 3, "q", 0),
+    ("mm", 3, "q", 1),
+    ("finish", 3, "kv"),
+    ("drain", 3, "q", 0, "S"),
+    ("mm", 3, "q", 2),
+    ("mm", 3, "q", 3),
+    ("drain", 3, "q", 1, "V"),
+    ("drain", 3, "q", 2, "S"),
+    ("tl", 3, "kv"),
+    ("drain", 3, "q", 3, "V"),
+    ("ll", 3, "kv"),
+    ("ql", 3, "kv"),
+    ("mm", 3, "kv", 0),
+    ("mm", 3, "kv", 1),
+    ("drain", 3, "kv", 0, "S"),
+    ("mm", 3, "kv", 2),
+    ("drain", 3, "kv", 1, "V"),
+    ("mm", 3, "kv", 3),
+    ("drain", 3, "kv", 2, "S"),
+    ("mm", 3, "kv", 4),
+    ("drain", 3, "kv", 3, "V"),
+    ("mm", 3, "kv", 5),
+    ("drain", 3, "kv", 4, "S"),
+    ("mm", 3, "kv", 6),
+    ("drain", 3, "kv", 5, "V"),
+    ("mm", 3, "kv", 7),
+    ("drain", 3, "kv", 6, "S"),
+    ("drain", 3, "kv", 7, "V"),
+]
+
+
+def tile_transformerdecoderblock_pa_w8_kernel(
+    tc, normed_bytes, normed_scale, w_dq, w_dq_s, q_g, q_b, w_uq, w_uq_s, w_dkv, w_dkv_s, kv_g, kv_b, w_ukv, w_ukv_s, out_q, out_kv
+):
+    nc = tc.nc
+    with ExitStack() as ctx:
+        keep = ctx.enter_context(tc.tile_pool(name="keep", bufs=1))
+        work = ctx.enter_context(tc.tile_pool(name="work", bufs=2))
+        psum = ctx.enter_context(tc.psum_pool(name="psum", bufs=2))
+        ctx.enter_context(tc.manual_schedule())
+
+        wsc = keep.tile([P, 2560], U8, align_bytes=64, name="wsc")
+        nc.vector.memset(wsc[:].bitcast(I32), 0)
+        rows = keep.tile([P, 4, LAT], BF16, name="rows")
+        nc.vector.memset(rows[:], 0.0)
+        ones = keep.tile([P, P], BF16, name="ones")
+        nc.vector.memset(ones[:], 1.0)
+        power = keep.tile([P, 1], F32, name="power")
+        nc.vector.memset(power[:], -0.5)
+        ident = keep.tile([P, P], F32, name="ident")
+        make_identity(nc, ident[:])
+
+        sc = keep.tile([P, PASSES, PACK], F32, name="sc")
+        nc.sync.dma_start(out=sc[:], in_=normed_scale.rearrange("a b (c p m) -> p (a b c) m", p=P, m=PACK))
+        x_bytes = [keep.tile([P, D], U8, name=f"x_bytes{i}") for i in range(B)]
+
+        def load_x(i):
+            nc.sync.dma_start(out=x_bytes[i][:], in_=normed_bytes[i])
+
+        dq = keep.tile([P, PASSES, LAT], U32, align_bytes=64, name="dq")
+        dkv = keep.tile([P, PASSES, LAT], U32, align_bytes=64, name="dkv")
+        uq = keep.tile([P, N_Q], U32, align_bytes=64, name="uq")
+        ukv = keep.tile([P, N_KV], U32, align_bytes=64, name="ukv")
+
+        def load_down(tile, w):
+            for g in range(0, PASSES, 2):
+                nc.sync.dma_start(out=tile[:, g:g + 2, :].bitcast(I32), in_=w[g:g + 2].rearrange("g p n t -> p g (n t)").bitcast(I32))
+
+        def load_up(tile, w, n):
+            words = w[0].rearrange("p n t -> p (n t)")
+            for c in range(0, n, 1024):
+                nc.sync.dma_start(out=tile[:, c:c + 1024].bitcast(I32), in_=words[:, 4 * c:4 * (c + 1024)].bitcast(I32))
+
+        def load_down_scales(col, s):
+            for q in range(4):
+                nc.sync.dma_start(out=wsc[32 * q:32 * q + 16, col:col + LAT].bitcast(I32), in_=s[:, 4 * q:4 * q + 4, :].bitcast(I32))
+
+        def load_up_scales(col, s, n):
+            w = n // 4
+            for q in range(4):
+                nc.sync.dma_start(out=wsc[32 * q:32 * q + 16, col:col + w].bitcast(I32), in_=s[0, 4 * q:4 * q + 4, :].rearrange("r (j n) -> j r n", j=4).bitcast(I32))
+
+        load_x(0)
+        load_x(1)
+        load_down(dkv, w_dkv)
+        load_down_scales(512, w_dkv_s)
+        load_x(3)
+        load_x(2)
+        for v, vec in enumerate((q_g, q_b, kv_g, kv_b)):
+            nc.sync.dma_start(out=rows[0:1, v, :], in_=vec.rearrange("(o n) -> o n", o=1))
+        load_down(dq, w_dq)
+        load_down_scales(0, w_dq_s)
+        load_up(ukv, w_ukv, N_KV)
+        load_up_scales(1536, w_ukv_s, N_KV)
+        load_up(uq, w_uq, N_Q)
+        load_up_scales(1024, w_uq_s, N_Q)
+
+        spread = [keep.tile([P, BANK], F32, name=f"spread{c}") for c in range(PASSES)]
+        for c in range(PASSES):
+            bank = psum.tile([P, PACK, P], F32, tag="bank", bufs=NB, name="bank")
+            for m in range(PACK):
+                nc.tensor.transpose(bank[:, m, :], sc[:, c, m:m + 1].to_broadcast([P, P]), ident[:])
+            src = bank[:].rearrange("p m n -> p n m")
+            dst = spread[c][:].rearrange("p (n m) -> p n m", m=PACK)
+            if c == 0:
+                nc.vector.tensor_copy(out=dst, in_=src)
+            else:
+                nc.scalar.copy(out=dst, in_=src)
+        affine = [keep.tile([P, LAT], F32, name=f"affine{v}") for v in range(4)]
+
+        abank = {}
+
+        def amm(v):
+            bank = psum.tile([P, LAT], F32, tag="turn", bufs=NT, name="bank")
+            nc.tensor.matmul(bank[:], lhsT=ones[:], rhs=rows[:, v, :], start=True, stop=True)
+            abank[v] = bank
+
+        def acopy(v):
+            nc.scalar.copy(out=affine[v][:], in_=abank[v][:])
+
+        xbank = {}
+        xb, xg, xq, xs = {}, {}, {}, {}
+
+        def widen(i, c):
+            if c == 0:
+                xb[i] = work.tile([P, D], BF16, tag="xb", bufs=4, name="xb")
+            cols = slice(c * K_PASS, (c + 1) * K_PASS)
+            nc.vector.tensor_tensor(out=xb[i][:, cols], in0=x_bytes[i][:, cols].bitcast(FP8), in1=spread[c][:], op=ALU.mult)
+
+        def turn(i, h):
+            bank = psum.tile([P, 2, 2, P], F32, tag="turn", bufs=NT, name="bank")
+            words = xb[i][:].bitcast(F32)
+            for g in range(2):
+                base = 256 * (2 * h + g)
+                for u in range(2):
+                    nc.tensor.transpose(bank[:, g, u, :], words[:, base + u:base + 256:2], ident[:])
+            xbank[i, h] = bank
+
+        def lay(i, h):
+            bank = xbank[i, h]
+            xg[i, h] = work.tile([P, 2, P, PACK], BF16, tag="xg", bufs=8, align_bytes=64, name="xg")
+            nc.scalar.copy(out=xg[i, h][:].rearrange("p g r t -> p (g r t)").bitcast(F32).rearrange("p (g r u) -> p g r u", g=2, u=2), in_=bank[:].rearrange("p g u r -> p g r u"))
+
+        def qx(i, h):
+            if h == 0:
+                xq[i] = keep.tile([P, PASSES, P], U32, align_bytes=64, name=f"xq{i}")
+                xs[i] = keep.tile([P, PASSES, P], U8, align_bytes=64, name=f"xs{i}")
+            g = slice(2 * h, 2 * h + 2)
+            nc.vector.quantize_mx(
+                out=xq[i][:, g, :].rearrange("p g r -> p (g r)").bitcast(FP8X4),
+                scales=xs[i][:, g, :].rearrange("p g r -> p (g r)"),
+                in_=xg[i, h][:].rearrange("p g r t -> p (g r t)"),
+            )
+
+        inv, lbank, obank = {}, {}, {}
+        lat, cen, stat, cn, cg, cq, cs = {}, {}, {}, {}, {}, {}, {}
+        down = {"q": (dq, 0, 0), "kv": (dkv, 512, 2)}
+        up = {"q": (uq, 1024, N_Q, out_q), "kv": (ukv, 1536, N_KV, out_kv)}
+
+        def project(i, path):
+            w, col, _ = down[path]
+            acc = psum.tile([P, LAT], F32, tag="lat", bufs=NL, name="lat")
+            for g in range(PASSES):
+                nc.tensor.matmul_mx(
+                    out=acc[:],
+                    lhsT=xq[i][:, g, :].bitcast(FP8X4),
+                    lhsT_scale=xs[i][:, g, :],
+                    rhs=w[:, g, :].bitcast(FP8X4),
+                    rhs_scale=wsc[4 * g:P, col:col + LAT],
+                    start=(g == 0),
+                    stop=(g == PASSES - 1),
+                )
+            lat[i, path] = acc
+
+        def stats(i, path):
+            six = work.tile([P, 6], F32, tag="six", bufs=8, name="six")
+            nc.vector.bn_stats(out=six[:], in_=lat[i, path][:])
+            stat[i, path] = six
+
+        def agg(i, path):
+            six = stat[i, path]
+            mv = work.tile([P, 2], F32, tag="mv", bufs=8, name="mv")
+            nc.vector.bn_aggr(out=mv[:], in_=six[:])
+            stat[i, path] = mv
+
+        def power_of(i, path):
+            mv = stat[i, path]
+            rstd = work.tile([P, 2], F32, tag="rstd", bufs=8, name="rstd")
+            nc.gpsimd.tensor_scalar(out=rstd[:, 0:1], in0=mv[:, 1:2], scalar1=EPS, scalar2=None, op0=ALU.add)
+            nc.gpsimd.tensor_tensor(out=rstd[:, 1:2], in0=rstd[:, 0:1], in1=power[:], op=ALU.pow)
+            inv[i, path] = rstd
+
+        def center(i, path):
+            mv = stat[i, path]
+            v = down[path][2]
+            t = work.tile([P, LAT], F32, tag="cen", bufs=8, name="cen")
+            nc.vector.scalar_tensor_tensor(out=t[:], in0=lat[i, path][:], scalar=mv[:, 0:1], in1=affine[v][:], op0=ALU.subtract, op1=ALU.mult)
+            cen[i, path] = t
+
+        def finish(i, path):
+            rstd = inv[i, path]
+            v = down[path][2]
+            t = work.tile([P, LAT], BF16, tag="cn", bufs=8, name="cn")
+            nc.vector.scalar_tensor_tensor(out=t[:], in0=cen[i, path][:], scalar=rstd[:, 1:2], in1=affine[v + 1][:], op0=ALU.mult, op1=ALU.add)
+            cn[i, path] = t
+
+        def tl(i, path):
+            bank = psum.tile([P, 2, P], F32, tag="turn", bufs=NT, name="bank")
+            words = cn[i, path][:].bitcast(F32)
+            for u in range(2):
+                nc.tensor.transpose(bank[:, u, :], words[:, u:256:2], ident[:])
+            lbank[i, path] = bank
+
+        def ll(i, path):
+            bank = lbank[i, path]
+            t = work.tile([P, P, PACK], BF16, tag="cg", bufs=8, align_bytes=64, name="cg")
+            nc.scalar.copy(out=t[:].rearrange("p r t -> p (r t)").bitcast(F32).rearrange("p (r u) -> p r u", u=2), in_=bank[:].rearrange("p u r -> p r u"))
+            cg[i, path] = t
+
+        def ql(i, path):
+            c = work.tile([P, P], U32, tag="cq", bufs=8, align_bytes=64, name="cq")
+            s = work.tile([P, P], U8, tag="cs", bufs=8, align_bytes=64, name="cs")
+            nc.vector.quantize_mx(out=c[:].bitcast(FP8X4), scales=s[:], in_=cg[i, path][:].rearrange("p r t -> p (r t)"))
+            cq[i, path] = (c, s)
+
+        res = {}
+
+        def mm(i, path, n):
+            w, col, width, out = up[path]
+            c, s = cq[i, path]
+            j, within = divmod(n * BANK, width // 4)
+            bank = psum.tile([P, BANK], F32, tag="bank", bufs=NB, name="bank")
+            nc.tensor.matmul_mx(
+                out=bank[:],
+                lhsT=c[:].bitcast(FP8X4),
+                lhsT_scale=s[:],
+                rhs=w[:, n * BANK:(n + 1) * BANK].bitcast(FP8X4),
+                rhs_scale=wsc[4 * j:P, col + within:col + within + BANK],
+                start=True,
+                stop=True,
+            )
+            obank[i, path, n] = bank
+
+        def drain(i, path, n, engine):
+            out = up[path][3]
+            bank = obank[i, path, n]
+            pair = (i, path, n // 2)
+            second = pair in res
+            if not second:
+                res[pair] = work.tile([P, 2, BANK], F32, tag="res", bufs=14, name="res")
+            dst = res[pair][:, n % 2, :]
+            if engine == "V":
+                nc.vector.tensor_copy(out=dst, in_=bank[:])
+            else:
+                nc.scalar.copy(out=dst, in_=bank[:])
+            if second:
+                m = n // 2 * 2
+                nc.sync.dma_start(out=out[i, :, m * BANK:(m + 2) * BANK], in_=res[pair][:].rearrange("p h n -> p (h n)"))
+
+        stages = {"widen": widen, "turn": turn, "lay": lay, "qx": qx, "project": project, "stats": stats, "agg": agg, "pow": power_of, "center": center, "finish": finish, "tl": tl, "ll": ll, "ql": ql, "mm": mm, "drain": drain, "amm": amm, "acopy": acopy}
+        for name, *args in ORDER:
+            stages[name](*args)

@@ -23,224 +23,235 @@ FP8 = mybir.dt.float8_e4m3fn
 FP8X4 = mybir.dt.float8_e4m3fn_x4
 ALU = mybir.AluOpType
 ACT = mybir.ActivationFunctionType
+GS = 2
+GCAST = ()
+LAST = (2, "q", 1)
 NB, NL, NT = 4, 2, 2
 ORDER = [
-    ("widen", 0, 0),
-    ("widen", 0, 1),
-    ("widen", 0, 2),
-    ("turn", 0, 0),
-    ("widen", 0, 3),
-    ("lay", 0, 0),
-    ("widen", 1, 0),
-    ("turn", 0, 1),
-    ("qx", 0, 0),
-    ("widen", 1, 1),
-    ("lay", 0, 1),
-    ("widen", 2, 0),
+    ("cast", 0, 0),
+    ("cast", 0, 1),
+    ("cast", 0, 3),
     ("amm", 2),
-    ("amm", 1),
-    ("qx", 0, 1),
+    ("cast", 0, 2),
+    ("turn", 0, 0),
     ("acopy", 2),
-    ("widen", 2, 1),
-    ("project", 0, "kv"),
-    ("acopy", 1),
-    ("widen", 2, 2),
-    ("widen", 2, 3),
-    ("amm", 3),
-    ("project", 0, "q"),
-    ("stats", 0, "kv"),
-    ("acopy", 3),
-    ("widen", 1, 2),
+    ("cast", 1, 0),
+    ("scale", 0, 1),
+    ("turn", 0, 1),
+    ("cast", 1, 3),
+    ("scale", 0, 0),
     ("amm", 0),
-    ("stats", 0, "q"),
-    ("turn", 2, 0),
+    ("cast", 1, 1),
+    ("scale", 0, 3),
+    ("cast", 1, 2),
+    ("qx", 0, 0),
+    ("scale", 0, 2),
     ("acopy", 0),
-    ("agg", 0, "kv"),
-    ("widen", 1, 3),
-    ("lay", 2, 0),
-    ("pow", 0, "kv"),
-    ("turn", 2, 1),
-    ("center", 0, "kv"),
     ("turn", 1, 0),
-    ("lay", 2, 1),
-    ("qx", 2, 0),
-    ("agg", 0, "q"),
-    ("lay", 1, 0),
-    ("finish", 0, "kv"),
+    ("qx", 0, 1),
     ("turn", 1, 1),
-    ("pow", 0, "q"),
-    ("center", 0, "q"),
-    ("tl", 0, "kv"),
-    ("lay", 1, 1),
-    ("qx", 2, 1),
-    ("ll", 0, "kv"),
-    ("finish", 0, "q"),
-    ("project", 2, "kv"),
+    ("scale", 1, 0),
+    ("project", 0, "kv"),
+    ("scale", 1, 1),
+    ("scale", 1, 3),
+    ("cast", 2, 0),
+    ("scale", 1, 2),
+    ("amm", 1),
+    ("cast", 2, 1),
+    ("amm", 3),
+    ("stats", 0, "kv"),
+    ("acopy", 1),
     ("qx", 1, 0),
-    ("ql", 0, "kv"),
+    ("agg", 0, "kv"),
+    ("acopy", 3),
     ("qx", 1, 1),
-    ("tl", 0, "q"),
-    ("widen", 3, 0),
-    ("mm", 0, "kv", 0),
-    ("ll", 0, "q"),
+    ("turn", 2, 0),
+    ("center", 0, "kv"),
+    ("pow", 0, "kv"),
+    ("cast", 2, 3),
     ("project", 1, "kv"),
-    ("stats", 2, "kv"),
-    ("drain", 0, "kv", 0, "S"),
-    ("ql", 0, "q"),
-    ("agg", 2, "kv"),
-    ("widen", 3, 1),
-    ("mm", 0, "kv", 1),
-    ("pow", 2, "kv"),
-    ("mm", 0, "q", 0),
-    ("drain", 0, "kv", 1, "S"),
+    ("finish", 0, "kv"),
+    ("cast", 3, 0),
+    ("scale", 2, 1),
+    ("cast", 2, 2),
+    ("tl", 0, "kv"),
+    ("cast", 3, 1),
     ("stats", 1, "kv"),
-    ("mm", 0, "q", 1),
-    ("mm", 0, "q", 2),
-    ("drain", 0, "q", 0, "S"),
+    ("turn", 2, 1),
+    ("ll", 0, "kv"),
+    ("scale", 2, 0),
+    ("cast", 3, 2),
+    ("ql", 0, "kv"),
     ("turn", 3, 0),
-    ("drain", 0, "q", 1, "V"),
-    ("drain", 0, "q", 2, "S"),
-    ("mm", 0, "q", 3),
     ("agg", 1, "kv"),
-    ("center", 2, "kv"),
-    ("mm", 0, "kv", 2),
+    ("scale", 2, 3),
     ("pow", 1, "kv"),
-    ("drain", 0, "q", 3, "S"),
+    ("mm", 0, "kv", 0),
+    ("scale", 2, 2),
+    ("mm", 0, "kv", 1),
+    ("mm", 0, "kv", 2),
+    ("drain", 0, "kv", 0, "S"),
+    ("qx", 2, 0),
     ("mm", 0, "kv", 3),
+    ("qx", 2, 1),
+    ("drain", 0, "kv", 1, "S"),
     ("center", 1, "kv"),
     ("mm", 0, "kv", 4),
     ("drain", 0, "kv", 2, "S"),
-    ("project", 1, "q"),
-    ("finish", 2, "kv"),
-    ("drain", 0, "kv", 3, "S"),
-    ("finish", 1, "kv"),
+    ("project", 2, "kv"),
+    ("drain", 0, "kv", 3, "V"),
     ("drain", 0, "kv", 4, "S"),
-    ("tl", 2, "kv"),
+    ("finish", 1, "kv"),
+    ("cast", 3, 3),
     ("mm", 0, "kv", 5),
-    ("stats", 1, "q"),
-    ("ll", 2, "kv"),
+    ("scale", 3, 1),
     ("mm", 0, "kv", 6),
-    ("mm", 0, "kv", 7),
     ("drain", 0, "kv", 5, "S"),
-    ("widen", 3, 2),
-    ("project", 2, "q"),
+    ("tl", 1, "kv"),
+    ("stats", 2, "kv"),
+    ("mm", 0, "kv", 7),
+    ("scale", 3, 0),
+    ("ll", 1, "kv"),
+    ("project", 0, "q"),
     ("drain", 0, "kv", 6, "S"),
-    ("agg", 1, "q"),
+    ("agg", 2, "kv"),
+    ("ql", 1, "kv"),
+    ("drain", 0, "kv", 7, "S"),
+    ("center", 2, "kv"),
+    ("mm", 1, "kv", 0),
+    ("pow", 2, "kv"),
+    ("mm", 1, "kv", 1),
+    ("stats", 0, "q"),
+    ("mm", 1, "kv", 2),
+    ("drain", 1, "kv", 0, "S"),
+    ("mm", 1, "kv", 3),
+    ("finish", 2, "kv"),
+    ("drain", 1, "kv", 1, "S"),
+    ("turn", 3, 1),
+    ("agg", 0, "q"),
+    ("drain", 1, "kv", 3, "V"),
+    ("drain", 1, "kv", 2, "S"),
+    ("tl", 2, "kv"),
+    ("center", 0, "q"),
+    ("mm", 1, "kv", 4),
+    ("pow", 0, "q"),
+    ("mm", 1, "kv", 5),
+    ("ll", 2, "kv"),
+    ("scale", 3, 2),
+    ("mm", 1, "kv", 6),
+    ("drain", 1, "kv", 4, "S"),
+    ("mm", 1, "kv", 7),
     ("ql", 2, "kv"),
+    ("project", 1, "q"),
+    ("drain", 1, "kv", 5, "S"),
+    ("scale", 3, 3),
+    ("drain", 1, "kv", 6, "S"),
+    ("qx", 3, 0),
+    ("finish", 0, "q"),
+    ("mm", 2, "kv", 0),
+    ("drain", 1, "kv", 7, "S"),
+    ("mm", 2, "kv", 1),
+    ("stats", 1, "q"),
+    ("mm", 2, "kv", 2),
+    ("drain", 2, "kv", 0, "S"),
+    ("tl", 0, "q"),
+    ("qx", 3, 1),
+    ("drain", 2, "kv", 1, "S"),
+    ("agg", 1, "q"),
+    ("mm", 2, "kv", 3),
+    ("drain", 2, "kv", 2, "V"),
+    ("mm", 2, "kv", 4),
+    ("ll", 0, "q"),
+    ("project", 3, "kv"),
     ("center", 1, "q"),
     ("pow", 1, "q"),
-    ("lay", 3, 0),
-    ("mm", 2, "kv", 0),
-    ("widen", 3, 3),
-    ("mm", 2, "kv", 1),
-    ("drain", 0, "kv", 7, "S"),
-    ("tl", 1, "kv"),
-    ("drain", 2, "kv", 0, "V"),
-    ("mm", 2, "kv", 2),
-    ("drain", 2, "kv", 1, "S"),
-    ("mm", 2, "kv", 3),
+    ("drain", 2, "kv", 3, "S"),
+    ("ql", 0, "q"),
+    ("drain", 2, "kv", 4, "S"),
     ("finish", 1, "q"),
-    ("turn", 3, 1),
-    ("ll", 1, "kv"),
-    ("drain", 2, "kv", 2, "S"),
-    ("drain", 2, "kv", 3, "V"),
-    ("mm", 2, "kv", 4),
-    ("tl", 1, "q"),
-    ("lay", 3, 1),
-    ("ql", 1, "kv"),
     ("mm", 2, "kv", 5),
-    ("drain", 2, "kv", 4, "V"),
-    ("mm", 2, "kv", 6),
-    ("ll", 1, "q"),
-    ("mm", 1, "kv", 0),
+    ("mm", 0, "q", 0),
+    ("stats", 3, "kv"),
+    ("mm", 0, "q", 1),
     ("drain", 2, "kv", 5, "S"),
-    ("qx", 3, 0),
-    ("mm", 1, "kv", 1),
-    ("drain", 1, "kv", 0, "V"),
-    ("drain", 2, "kv", 6, "S"),
-    ("mm", 1, "kv", 2),
-    ("drain", 1, "kv", 1, "V"),
-    ("drain", 1, "kv", 2, "S"),
-    ("mm", 1, "kv", 3),
-    ("ql", 1, "q"),
-    ("mm", 1, "kv", 4),
-    ("qx", 3, 1),
-    ("drain", 1, "kv", 3, "S"),
-    ("mm", 1, "kv", 5),
-    ("stats", 2, "q"),
-    ("mm", 1, "q", 0),
-    ("drain", 1, "kv", 4, "S"),
+    ("tl", 1, "q"),
+    ("drain", 0, "q", 0, "V"),
+    ("drain", 0, "q", 1, "S"),
+    ("mm", 0, "q", 2),
+    ("agg", 3, "kv"),
+    ("mm", 0, "q", 3),
+    ("ll", 1, "q"),
     ("project", 3, "q"),
-    ("drain", 1, "kv", 5, "V"),
-    ("drain", 1, "q", 0, "S"),
-    ("agg", 2, "q"),
-    ("center", 2, "q"),
-    ("pow", 2, "q"),
-    ("mm", 1, "kv", 6),
-    ("mm", 1, "q", 1),
-    ("drain", 1, "kv", 6, "S"),
+    ("center", 3, "kv"),
+    ("pow", 3, "kv"),
+    ("drain", 0, "q", 2, "S"),
+    ("ql", 1, "q"),
+    ("finish", 3, "kv"),
+    ("drain", 0, "q", 3, "S"),
+    ("mm", 2, "kv", 6),
+    ("mm", 2, "kv", 7),
     ("stats", 3, "q"),
-    ("mm", 1, "kv", 7),
-    ("mm", 1, "q", 2),
-    ("drain", 1, "q", 1, "S"),
-    ("drain", 1, "kv", 7, "V"),
-    ("project", 3, "kv"),
-    ("drain", 1, "q", 2, "S"),
+    ("mm", 1, "q", 0),
+    ("drain", 2, "kv", 6, "S"),
+    ("drain", 2, "kv", 7, "V"),
+    ("tl", 3, "kv"),
+    ("drain", 1, "q", 0, "S"),
+    ("mm", 1, "q", 1),
     ("agg", 3, "q"),
-    ("finish", 2, "q"),
-    ("pow", 3, "q"),
+    ("mm", 1, "q", 2),
+    ("ll", 3, "kv"),
     ("mm", 1, "q", 3),
     ("center", 3, "q"),
-    ("mm", 2, "kv", 7),
-    ("drain", 1, "q", 3, "S"),
-    ("tl", 2, "q"),
-    ("stats", 3, "kv"),
-    ("ll", 2, "q"),
-    ("finish", 3, "q"),
-    ("drain", 2, "kv", 7, "S"),
-    ("agg", 3, "kv"),
-    ("ql", 2, "q"),
-    ("tl", 3, "q"),
-    ("pow", 3, "kv"),
-    ("center", 3, "kv"),
-    ("mm", 2, "q", 0),
-    ("ll", 3, "q"),
-    ("mm", 2, "q", 1),
-    ("drain", 2, "q", 0, "V"),
-    ("mm", 2, "q", 2),
-    ("drain", 2, "q", 1, "S"),
-    ("mm", 2, "q", 3),
-    ("ql", 3, "q"),
-    ("drain", 2, "q", 2, "V"),
-    ("drain", 2, "q", 3, "S"),
-    ("mm", 3, "q", 0),
-    ("mm", 3, "q", 1),
-    ("finish", 3, "kv"),
-    ("drain", 3, "q", 0, "S"),
-    ("mm", 3, "q", 2),
-    ("mm", 3, "q", 3),
-    ("drain", 3, "q", 1, "V"),
-    ("drain", 3, "q", 2, "S"),
-    ("tl", 3, "kv"),
-    ("drain", 3, "q", 3, "V"),
-    ("ll", 3, "kv"),
+    ("drain", 1, "q", 1, "S"),
+    ("project", 2, "q"),
     ("ql", 3, "kv"),
+    ("pow", 3, "q"),
+    ("drain", 1, "q", 2, "V"),
+    ("drain", 1, "q", 3, "S"),
+    ("finish", 3, "q"),
     ("mm", 3, "kv", 0),
     ("mm", 3, "kv", 1),
-    ("drain", 3, "kv", 0, "S"),
+    ("stats", 2, "q"),
     ("mm", 3, "kv", 2),
-    ("drain", 3, "kv", 1, "V"),
+    ("drain", 3, "kv", 0, "S"),
     ("mm", 3, "kv", 3),
+    ("drain", 3, "kv", 1, "V"),
     ("drain", 3, "kv", 2, "S"),
+    ("tl", 3, "q"),
+    ("agg", 2, "q"),
     ("mm", 3, "kv", 4),
     ("drain", 3, "kv", 3, "V"),
+    ("ll", 3, "q"),
     ("mm", 3, "kv", 5),
-    ("drain", 3, "kv", 4, "S"),
+    ("pow", 2, "q"),
     ("mm", 3, "kv", 6),
-    ("drain", 3, "kv", 5, "V"),
+    ("center", 2, "q"),
+    ("drain", 3, "kv", 4, "S"),
     ("mm", 3, "kv", 7),
-    ("drain", 3, "kv", 6, "S"),
-    ("drain", 3, "kv", 7, "V"),
+    ("ql", 3, "q"),
+    ("drain", 3, "kv", 5, "S"),
+    ("finish", 2, "q"),
+    ("mm", 3, "q", 0),
+    ("drain", 3, "kv", 7, "S"),
+    ("drain", 3, "kv", 6, "V"),
+    ("mm", 3, "q", 1),
+    ("drain", 3, "q", 0, "S"),
+    ("tl", 2, "q"),
+    ("drain", 3, "q", 1, "V"),
+    ("mm", 3, "q", 2),
+    ("ll", 2, "q"),
+    ("mm", 3, "q", 3),
+    ("drain", 3, "q", 2, "S"),
+    ("ql", 2, "q"),
+    ("drain", 3, "q", 3, "V"),
+    ("mm", 2, "q", 0),
+    ("mm", 2, "q", 1),
+    ("mm", 2, "q", 2),
+    ("drain", 2, "q", 0, "V"),
+    ("mm", 2, "q", 3),
+    ("drain", 2, "q", 1, "S"),
+    ("drain", 2, "q", 2, "V"),
+    ("drain", 2, "q", 3, "S"),
 ]
 
 
@@ -254,14 +265,20 @@ def tile_transformerdecoderblock_pa_w8_kernel(
         psum = ctx.enter_context(tc.psum_pool(name="psum", bufs=2))
         ctx.enter_context(tc.manual_schedule())
 
+        rows = keep.tile([P, 4, LAT], BF16, name="rows")
+        nc.vector.memset(rows[:].rearrange("p v n -> p (v n)").bitcast(F32), 0.0)
         wsc = keep.tile([P, 2560], U8, align_bytes=64, name="wsc")
         nc.vector.memset(wsc[:].bitcast(I32), 0)
-        rows = keep.tile([P, 4, LAT], BF16, name="rows")
-        nc.vector.memset(rows[:], 0.0)
         ones = keep.tile([P, P], BF16, name="ones")
         nc.vector.memset(ones[:], 1.0)
-        power = keep.tile([P, 1], F32, name="power")
-        nc.vector.memset(power[:], -0.5)
+        for v, vec in enumerate((q_g, q_b, kv_g, kv_b)):
+            nc.scalar.dma_start(out=rows[0:1, v, :], in_=vec.rearrange("(o n) -> o n", o=1))
+        zero = keep.tile([P, 1], F32, name="zero")
+        nc.vector.memset(zero[:], 0.0)
+        eps = keep.tile([P, 1], F32, name="eps")
+        nc.vector.tensor_scalar(out=eps[:], in0=zero[:], scalar1=EPS, scalar2=None, op0=ALU.add)
+        dummy = keep.tile([P, 1], F32, name="dummy")
+        nc.scalar.activation(out=dummy[:], in_=eps[:], func=ACT.Abs_reciprocal_sqrt)
         ident = keep.tile([P, P], F32, name="ident")
         make_identity(nc, ident[:])
 
@@ -278,13 +295,11 @@ def tile_transformerdecoderblock_pa_w8_kernel(
         ukv = keep.tile([P, N_KV], U32, align_bytes=64, name="ukv")
 
         def load_down(tile, w):
-            for g in range(0, PASSES, 2):
-                nc.sync.dma_start(out=tile[:, g:g + 2, :].bitcast(I32), in_=w[g:g + 2].rearrange("g p n t -> p g (n t)").bitcast(I32))
+            nc.sync.dma_start(out=tile[:].bitcast(I32), in_=w.rearrange("g p n t -> p g (n t)").bitcast(I32))
 
-        def load_up(tile, w, n):
+        def load_up(tile, w, c):
             words = w[0].rearrange("p n t -> p (n t)")
-            for c in range(0, n, 1024):
-                nc.sync.dma_start(out=tile[:, c:c + 1024].bitcast(I32), in_=words[:, 4 * c:4 * (c + 1024)].bitcast(I32))
+            nc.sync.dma_start(out=tile[:, c:c + 2048].bitcast(I32), in_=words[:, 4 * c:4 * (c + 2048)].bitcast(I32))
 
         def load_down_scales(col, s):
             for q in range(4):
@@ -297,30 +312,18 @@ def tile_transformerdecoderblock_pa_w8_kernel(
 
         load_x(0)
         load_x(1)
-        load_down(dkv, w_dkv)
         load_down_scales(512, w_dkv_s)
-        load_x(3)
-        load_x(2)
-        for v, vec in enumerate((q_g, q_b, kv_g, kv_b)):
-            nc.sync.dma_start(out=rows[0:1, v, :], in_=vec.rearrange("(o n) -> o n", o=1))
-        load_down(dq, w_dq)
-        load_down_scales(0, w_dq_s)
-        load_up(ukv, w_ukv, N_KV)
+        load_down(dkv, w_dkv)
         load_up_scales(1536, w_ukv_s, N_KV)
-        load_up(uq, w_uq, N_Q)
+        load_up(ukv, w_ukv, 0)
+        load_x(2)
+        load_up(ukv, w_ukv, 2048)
+        load_x(3)
+        load_down_scales(0, w_dq_s)
         load_up_scales(1024, w_uq_s, N_Q)
+        load_down(dq, w_dq)
+        load_up(uq, w_uq, 0)
 
-        spread = [keep.tile([P, BANK], F32, name=f"spread{c}") for c in range(PASSES)]
-        for c in range(PASSES):
-            bank = psum.tile([P, PACK, P], F32, tag="bank", bufs=NB, name="bank")
-            for m in range(PACK):
-                nc.tensor.transpose(bank[:, m, :], sc[:, c, m:m + 1].to_broadcast([P, P]), ident[:])
-            src = bank[:].rearrange("p m n -> p n m")
-            dst = spread[c][:].rearrange("p (n m) -> p n m", m=PACK)
-            if c == 0:
-                nc.vector.tensor_copy(out=dst, in_=src)
-            else:
-                nc.scalar.copy(out=dst, in_=src)
         affine = [keep.tile([P, LAT], F32, name=f"affine{v}") for v in range(4)]
 
         abank = {}
@@ -336,11 +339,17 @@ def tile_transformerdecoderblock_pa_w8_kernel(
         xbank = {}
         xb, xg, xq, xs = {}, {}, {}, {}
 
-        def widen(i, c):
-            if c == 0:
+        def cast(i, c):
+            if i not in xb:
                 xb[i] = work.tile([P, D], BF16, tag="xb", bufs=4, name="xb")
             cols = slice(c * K_PASS, (c + 1) * K_PASS)
-            nc.vector.tensor_tensor(out=xb[i][:, cols], in0=x_bytes[i][:, cols].bitcast(FP8), in1=spread[c][:], op=ALU.mult)
+            src = x_bytes[i][:, cols].bitcast(FP8)
+            if i in GCAST:
+                nc.gpsimd.tensor_copy(out=xb[i][:, cols], in_=src)
+            elif i == 0 and c % 2 == 1:
+                nc.vector.tensor_copy(out=xb[i][:, cols], in_=src)
+            else:
+                nc.scalar.copy(out=xb[i][:, cols], in_=src)
 
         def turn(i, h):
             bank = psum.tile([P, 2, 2, P], F32, tag="turn", bufs=NT, name="bank")
@@ -351,26 +360,32 @@ def tile_transformerdecoderblock_pa_w8_kernel(
                     nc.tensor.transpose(bank[:, g, u, :], words[:, base + u:base + 256:2], ident[:])
             xbank[i, h] = bank
 
-        def lay(i, h):
-            bank = xbank[i, h]
-            xg[i, h] = work.tile([P, 2, P, PACK], BF16, tag="xg", bufs=8, align_bytes=64, name="xg")
-            nc.scalar.copy(out=xg[i, h][:].rearrange("p g r t -> p (g r t)").bitcast(F32).rearrange("p (g r u) -> p g r u", g=2, u=2), in_=bank[:].rearrange("p g u r -> p g r u"))
+        def scale(i, c):
+            h, g = divmod(c, 2)
+            if i not in xg:
+                xg[i] = work.tile([P, PASSES, P, PACK], BF16, tag="xg", bufs=4, align_bytes=64, name="xg")
+            nc.vector.tensor_tensor(
+                out=xg[i][:, c].rearrange("p r (u e) -> p r u e", e=2),
+                in0=xbank[i, h][:, g].bitcast(BF16).rearrange("p u (r e) -> p r u e", e=2),
+                in1=sc[:, c, :].rearrange("p (u e) -> p u e", e=2).unsqueeze(1).to_broadcast([P, P, 2, 2]),
+                op=ALU.mult,
+            )
 
         def qx(i, h):
-            if h == 0:
+            if i not in xq:
                 xq[i] = keep.tile([P, PASSES, P], U32, align_bytes=64, name=f"xq{i}")
                 xs[i] = keep.tile([P, PASSES, P], U8, align_bytes=64, name=f"xs{i}")
-            g = slice(2 * h, 2 * h + 2)
+            g = slice(0, PASSES) if h == 2 else slice(2 * h, 2 * h + 2)
             nc.vector.quantize_mx(
                 out=xq[i][:, g, :].rearrange("p g r -> p (g r)").bitcast(FP8X4),
                 scales=xs[i][:, g, :].rearrange("p g r -> p (g r)"),
-                in_=xg[i, h][:].rearrange("p g r t -> p (g r t)"),
+                in_=xg[i][:, g].rearrange("p g r t -> p (g r t)"),
             )
 
-        inv, lbank, obank = {}, {}, {}
-        lat, cen, stat, cn, cg, cq, cs = {}, {}, {}, {}, {}, {}, {}
         down = {"q": (dq, 0, 0), "kv": (dkv, 512, 2)}
         up = {"q": (uq, 1024, N_Q, out_q), "kv": (ukv, 1536, N_KV, out_kv)}
+        half = {"kv": (0, 1), "q": (1, 2), "j": (0, 2)}
+        lat, cen, mv, inv, cn, cg, cq, cs, lbank, obank, six = ({} for v in range(11))
 
         def project(i, path):
             w, col, _ = down[path]
@@ -388,67 +403,72 @@ def tile_transformerdecoderblock_pa_w8_kernel(
             lat[i, path] = acc
 
         def stats(i, path):
-            six = work.tile([P, 6], F32, tag="six", bufs=8, name="six")
-            nc.vector.bn_stats(out=six[:], in_=lat[i, path][:])
-            stat[i, path] = six
+            t = work.tile([P, 6], F32, tag="six", bufs=8, name="six")
+            nc.vector.bn_stats(out=t[:], in_=lat[i, path][:])
+            six[i, path] = t
 
         def agg(i, path):
-            six = stat[i, path]
-            mv = work.tile([P, 2], F32, tag="mv", bufs=8, name="mv")
-            nc.vector.bn_aggr(out=mv[:], in_=six[:])
-            stat[i, path] = mv
+            if i not in mv:
+                mv[i] = work.tile([P, 2, 2], F32, tag="mv", bufs=4, name="mv")
+                inv[i] = work.tile([P, 2], F32, tag="inv", bufs=4, name="inv")
+                cn[i] = work.tile([P, 2, LAT], BF16, tag="cn", bufs=4, name="cn")
+                cg[i] = work.tile([P, 2, P, PACK], BF16, tag="cg", bufs=4, align_bytes=64, name="cg")
+                cq[i] = work.tile([P, 2, P], U32, tag="cq", bufs=4, align_bytes=64, name="cq")
+                cs[i] = work.tile([P, 2, P], U8, tag="cs", bufs=4, align_bytes=64, name="cs")
+            a, b = half[path]
+            nc.vector.bn_aggr(out=mv[i][:, a, :], in_=six[i, path][:])
 
         def power_of(i, path):
-            mv = stat[i, path]
-            rstd = work.tile([P, 2], F32, tag="rstd", bufs=8, name="rstd")
-            nc.gpsimd.tensor_scalar(out=rstd[:, 0:1], in0=mv[:, 1:2], scalar1=EPS, scalar2=None, op0=ALU.add)
-            nc.gpsimd.tensor_tensor(out=rstd[:, 1:2], in0=rstd[:, 0:1], in1=power[:], op=ALU.pow)
-            inv[i, path] = rstd
+            a, b = half[path]
+            nc.scalar.activation(out=inv[i][:, a:b], in_=mv[i][:, a:b, 1], func=ACT.Abs_reciprocal_sqrt, bias=eps[:], scale=1.0)
 
         def center(i, path):
-            mv = stat[i, path]
+            a, b = half[path]
             v = down[path][2]
             t = work.tile([P, LAT], F32, tag="cen", bufs=8, name="cen")
-            nc.vector.scalar_tensor_tensor(out=t[:], in0=lat[i, path][:], scalar=mv[:, 0:1], in1=affine[v][:], op0=ALU.subtract, op1=ALU.mult)
+            nc.vector.scalar_tensor_tensor(out=t[:], in0=lat[i, path][:], scalar=mv[i][:, a, 0:1], in1=affine[v][:], op0=ALU.subtract, op1=ALU.mult)
             cen[i, path] = t
 
         def finish(i, path):
-            rstd = inv[i, path]
+            a, b = half[path]
             v = down[path][2]
-            t = work.tile([P, LAT], BF16, tag="cn", bufs=8, name="cn")
-            nc.vector.scalar_tensor_tensor(out=t[:], in0=cen[i, path][:], scalar=rstd[:, 1:2], in1=affine[v + 1][:], op0=ALU.mult, op1=ALU.add)
-            cn[i, path] = t
+            nc.vector.scalar_tensor_tensor(out=cn[i][:, a, :], in0=cen[i, path][:], scalar=inv[i][:, a:b], in1=affine[v + 1][:], op0=ALU.mult, op1=ALU.add)
 
         def tl(i, path):
-            bank = psum.tile([P, 2, P], F32, tag="turn", bufs=NT, name="bank")
-            words = cn[i, path][:].bitcast(F32)
-            for u in range(2):
-                nc.tensor.transpose(bank[:, u, :], words[:, u:256:2], ident[:])
+            a, b = half[path]
+            bank = psum.tile([P, 2, 2, P], F32, tag="turn", bufs=NT, name="bank")
+            for k in range(a, b):
+                words = cn[i][:, k, :].bitcast(F32)
+                for u in range(2):
+                    nc.tensor.transpose(bank[:, k, u, :], words[:, u:256:2], ident[:])
             lbank[i, path] = bank
 
         def ll(i, path):
-            bank = lbank[i, path]
-            t = work.tile([P, P, PACK], BF16, tag="cg", bufs=8, align_bytes=64, name="cg")
-            nc.scalar.copy(out=t[:].rearrange("p r t -> p (r t)").bitcast(F32).rearrange("p (r u) -> p r u", u=2), in_=bank[:].rearrange("p u r -> p r u"))
-            cg[i, path] = t
+            a, b = half[path]
+            nc.scalar.copy(
+                out=cg[i][:, a:b].rearrange("p k r t -> p k (r t)").bitcast(F32).rearrange("p k (r u) -> p k r u", u=2),
+                in_=lbank[i, path][:, a:b].rearrange("p k u r -> p k r u"),
+            )
 
         def ql(i, path):
-            c = work.tile([P, P], U32, tag="cq", bufs=8, align_bytes=64, name="cq")
-            s = work.tile([P, P], U8, tag="cs", bufs=8, align_bytes=64, name="cs")
-            nc.vector.quantize_mx(out=c[:].bitcast(FP8X4), scales=s[:], in_=cg[i, path][:].rearrange("p r t -> p (r t)"))
-            cq[i, path] = (c, s)
+            a, b = half[path]
+            nc.vector.quantize_mx(
+                out=cq[i][:, a:b, :].rearrange("p k r -> p (k r)").bitcast(FP8X4),
+                scales=cs[i][:, a:b, :].rearrange("p k r -> p (k r)"),
+                in_=cg[i][:, a:b].rearrange("p k r t -> p (k r t)"),
+            )
 
         res = {}
 
         def mm(i, path, n):
             w, col, width, out = up[path]
-            c, s = cq[i, path]
+            a, b = half[path]
             j, within = divmod(n * BANK, width // 4)
             bank = psum.tile([P, BANK], F32, tag="bank", bufs=NB, name="bank")
             nc.tensor.matmul_mx(
                 out=bank[:],
-                lhsT=c[:].bitcast(FP8X4),
-                lhsT_scale=s[:],
+                lhsT=cq[i][:, a, :].bitcast(FP8X4),
+                lhsT_scale=cs[i][:, a, :],
                 rhs=w[:, n * BANK:(n + 1) * BANK].bitcast(FP8X4),
                 rhs_scale=wsc[4 * j:P, col + within:col + within + BANK],
                 start=True,
@@ -458,20 +478,22 @@ def tile_transformerdecoderblock_pa_w8_kernel(
 
         def drain(i, path, n, engine):
             out = up[path][3]
-            bank = obank[i, path, n]
-            pair = (i, path, n // 2)
-            second = pair in res
-            if not second:
-                res[pair] = work.tile([P, 2, BANK], F32, tag="res", bufs=14, name="res")
-            dst = res[pair][:, n % 2, :]
+            four = (i, path, n // GS)
+            if four not in res:
+                res[four] = [work.tile([P, GS, BANK], F32, tag="res", bufs=28 // GS, name="res"), 0]
+            tile = res[four][0]
+            dst = tile[:, n % GS, :]
             if engine == "V":
-                nc.vector.tensor_copy(out=dst, in_=bank[:])
+                nc.vector.tensor_copy(out=dst, in_=obank[i, path, n][:])
             else:
-                nc.scalar.copy(out=dst, in_=bank[:])
-            if second:
-                m = n // 2 * 2
-                nc.sync.dma_start(out=out[i, :, m * BANK:(m + 2) * BANK], in_=res[pair][:].rearrange("p h n -> p (h n)"))
+                nc.scalar.copy(out=dst, in_=obank[i, path, n][:])
+            res[four][1] += 1
+            m = n // GS * GS
+            if four == LAST:
+                nc.sync.dma_start(out=out[i, :, n * BANK:(n + 1) * BANK], in_=dst)
+            elif res[four][1] == GS:
+                nc.sync.dma_start(out=out[i, :, m * BANK:(m + GS) * BANK], in_=tile[:].rearrange("p h n -> p (h n)"))
 
-        stages = {"widen": widen, "turn": turn, "lay": lay, "qx": qx, "project": project, "stats": stats, "agg": agg, "pow": power_of, "center": center, "finish": finish, "tl": tl, "ll": ll, "ql": ql, "mm": mm, "drain": drain, "amm": amm, "acopy": acopy}
+        stages = {"cast": cast, "turn": turn, "scale": scale, "qx": qx, "project": project, "stats": stats, "agg": agg, "pow": power_of, "center": center, "finish": finish, "tl": tl, "ll": ll, "ql": ql, "mm": mm, "drain": drain, "amm": amm, "acopy": acopy}
         for name, *args in ORDER:
             stages[name](*args)

from contextlib import ExitStack

import concourse.mybir as mybir
from concourse.masks import make_identity

B, S, D, LAT = 4, 128, 2048, 512
N_Q, N_KV = 2048, 4096
EPS = 1e-5
FLOPS = 2 * B * S * D * (LAT + LAT) + 2 * B * S * LAT * (N_Q + N_KV)

P = 128
PACK = 4
K_PASS = 512
PASSES = D // K_PASS
BANK = 512

F32 = mybir.dt.float32
BF16 = mybir.dt.bfloat16
U32 = mybir.dt.uint32
U8 = mybir.dt.uint8
I32 = mybir.dt.int32
FP8 = mybir.dt.float8_e4m3fn
FP8X4 = mybir.dt.float8_e4m3fn_x4
ALU = mybir.AluOpType
ACT = mybir.ActivationFunctionType
GS = 2
GCAST = ()
LAST = (2, "q", 1)
NB, NL, NT = 4, 2, 2
ORDER = [
    ("cast", 0, 0),
    ("cast", 0, 1),
    ("cast", 0, 3),
    ("amm", 2),
    ("cast", 0, 2),
    ("turn", 0, 0),
    ("acopy", 2),
    ("cast", 1, 0),
    ("scale", 0, 1),
    ("turn", 0, 1),
    ("cast", 1, 3),
    ("scale", 0, 0),
    ("amm", 0),
    ("cast", 1, 1),
    ("scale", 0, 3),
    ("cast", 1, 2),
    ("qx", 0, 0),
    ("scale", 0, 2),
    ("acopy", 0),
    ("turn", 1, 0),
    ("qx", 0, 1),
    ("turn", 1, 1),
    ("scale", 1, 0),
    ("project", 0, "kv"),
    ("scale", 1, 1),
    ("scale", 1, 3),
    ("cast", 2, 0),
    ("scale", 1, 2),
    ("amm", 1),
    ("cast", 2, 1),
    ("amm", 3),
    ("stats", 0, "kv"),
    ("acopy", 1),
    ("qx", 1, 0),
    ("agg", 0, "kv"),
    ("acopy", 3),
    ("qx", 1, 1),
    ("turn", 2, 0),
    ("center", 0, "kv"),
    ("pow", 0, "kv"),
    ("cast", 2, 3),
    ("project", 1, "kv"),
    ("finish", 0, "kv"),
    ("cast", 3, 0),
    ("scale", 2, 1),
    ("cast", 2, 2),
    ("tl", 0, "kv"),
    ("cast", 3, 1),
    ("stats", 1, "kv"),
    ("turn", 2, 1),
    ("ll", 0, "kv"),
    ("scale", 2, 0),
    ("cast", 3, 2),
    ("ql", 0, "kv"),
    ("turn", 3, 0),
    ("agg", 1, "kv"),
    ("scale", 2, 3),
    ("pow", 1, "kv"),
    ("mm", 0, "kv", 0),
    ("scale", 2, 2),
    ("mm", 0, "kv", 1),
    ("mm", 0, "kv", 2),
    ("drain", 0, "kv", 0, "S"),
    ("qx", 2, 0),
    ("mm", 0, "kv", 3),
    ("qx", 2, 1),
    ("drain", 0, "kv", 1, "S"),
    ("center", 1, "kv"),
    ("mm", 0, "kv", 4),
    ("drain", 0, "kv", 2, "S"),
    ("project", 2, "kv"),
    ("drain", 0, "kv", 3, "V"),
    ("drain", 0, "kv", 4, "S"),
    ("finish", 1, "kv"),
    ("cast", 3, 3),
    ("mm", 0, "kv", 5),
    ("scale", 3, 1),
    ("mm", 0, "kv", 6),
    ("drain", 0, "kv", 5, "S"),
    ("tl", 1, "kv"),
    ("stats", 2, "kv"),
    ("mm", 0, "kv", 7),
    ("scale", 3, 0),
    ("ll", 1, "kv"),
    ("project", 0, "q"),
    ("drain", 0, "kv", 6, "S"),
    ("agg", 2, "kv"),
    ("ql", 1, "kv"),
    ("drain", 0, "kv", 7, "S"),
    ("center", 2, "kv"),
    ("mm", 1, "kv", 0),
    ("pow", 2, "kv"),
    ("mm", 1, "kv", 1),
    ("stats", 0, "q"),
    ("mm", 1, "kv", 2),
    ("drain", 1, "kv", 0, "S"),
    ("mm", 1, "kv", 3),
    ("finish", 2, "kv"),
    ("drain", 1, "kv", 1, "S"),
    ("turn", 3, 1),
    ("agg", 0, "q"),
    ("drain", 1, "kv", 3, "V"),
    ("drain", 1, "kv", 2, "S"),
    ("tl", 2, "kv"),
    ("center", 0, "q"),
    ("mm", 1, "kv", 4),
    ("pow", 0, "q"),
    ("mm", 1, "kv", 5),
    ("ll", 2, "kv"),
    ("scale", 3, 2),
    ("mm", 1, "kv", 6),
    ("drain", 1, "kv", 4, "S"),
    ("mm", 1, "kv", 7),
    ("ql", 2, "kv"),
    ("project", 1, "q"),
    ("drain", 1, "kv", 5, "S"),
    ("scale", 3, 3),
    ("drain", 1, "kv", 6, "S"),
    ("qx", 3, 0),
    ("finish", 0, "q"),
    ("mm", 2, "kv", 0),
    ("drain", 1, "kv", 7, "S"),
    ("mm", 2, "kv", 1),
    ("stats", 1, "q"),
    ("mm", 2, "kv", 2),
    ("drain", 2, "kv", 0, "S"),
    ("tl", 0, "q"),
    ("qx", 3, 1),
    ("drain", 2, "kv", 1, "S"),
    ("agg", 1, "q"),
    ("mm", 2, "kv", 3),
    ("drain", 2, "kv", 2, "V"),
    ("mm", 2, "kv", 4),
    ("ll", 0, "q"),
    ("project", 3, "kv"),
    ("center", 1, "q"),
    ("pow", 1, "q"),
    ("drain", 2, "kv", 3, "S"),
    ("ql", 0, "q"),
    ("drain", 2, "kv", 4, "S"),
    ("finish", 1, "q"),
    ("mm", 2, "kv", 5),
    ("mm", 0, "q", 0),
    ("stats", 3, "kv"),
    ("mm", 0, "q", 1),
    ("drain", 2, "kv", 5, "S"),
    ("tl", 1, "q"),
    ("drain", 0, "q", 0, "V"),
    ("drain", 0, "q", 1, "S"),
    ("mm", 0, "q", 2),
    ("agg", 3, "kv"),
    ("mm", 0, "q", 3),
    ("ll", 1, "q"),
    ("project", 3, "q"),
    ("center", 3, "kv"),
    ("pow", 3, "kv"),
    ("drain", 0, "q", 2, "S"),
    ("ql", 1, "q"),
    ("finish", 3, "kv"),
    ("drain", 0, "q", 3, "S"),
    ("mm", 2, "kv", 6),
    ("mm", 2, "kv", 7),
    ("stats", 3, "q"),
    ("mm", 1, "q", 0),
    ("drain", 2, "kv", 6, "S"),
    ("drain", 2, "kv", 7, "V"),
    ("tl", 3, "kv"),
    ("drain", 1, "q", 0, "S"),
    ("mm", 1, "q", 1),
    ("agg", 3, "q"),
    ("mm", 1, "q", 2),
    ("ll", 3, "kv"),
    ("mm", 1, "q", 3),
    ("center", 3, "q"),
    ("drain", 1, "q", 1, "S"),
    ("project", 2, "q"),
    ("ql", 3, "kv"),
    ("pow", 3, "q"),
    ("drain", 1, "q", 2, "V"),
    ("drain", 1, "q", 3, "S"),
    ("finish", 3, "q"),
    ("mm", 3, "kv", 0),
    ("mm", 3, "kv", 1),
    ("stats", 2, "q"),
    ("mm", 3, "kv", 2),
    ("drain", 3, "kv", 0, "S"),
    ("mm", 3, "kv", 3),
    ("drain", 3, "kv", 1, "V"),
    ("drain", 3, "kv", 2, "S"),
    ("tl", 3, "q"),
    ("agg", 2, "q"),
    ("mm", 3, "kv", 4),
    ("drain", 3, "kv", 3, "V"),
    ("ll", 3, "q"),
    ("mm", 3, "kv", 5),
    ("pow", 2, "q"),
    ("mm", 3, "kv", 6),
    ("center", 2, "q"),
    ("drain", 3, "kv", 4, "S"),
    ("mm", 3, "kv", 7),
    ("ql", 3, "q"),
    ("drain", 3, "kv", 5, "S"),
    ("finish", 2, "q"),
    ("mm", 3, "q", 0),
    ("drain", 3, "kv", 7, "S"),
    ("drain", 3, "kv", 6, "V"),
    ("mm", 3, "q", 1),
    ("drain", 3, "q", 0, "S"),
    ("tl", 2, "q"),
    ("drain", 3, "q", 1, "V"),
    ("mm", 3, "q", 2),
    ("ll", 2, "q"),
    ("mm", 3, "q", 3),
    ("drain", 3, "q", 2, "S"),
    ("ql", 2, "q"),
    ("drain", 3, "q", 3, "V"),
    ("mm", 2, "q", 0),
    ("mm", 2, "q", 1),
    ("mm", 2, "q", 2),
    ("drain", 2, "q", 0, "V"),
    ("mm", 2, "q", 3),
    ("drain", 2, "q", 1, "S"),
    ("drain", 2, "q", 2, "V"),
    ("drain", 2, "q", 3, "S"),
]


def tile_transformerdecoderblock_pa_w8_kernel(
    tc, normed_bytes, normed_scale, w_dq, w_dq_s, q_g, q_b, w_uq, w_uq_s, w_dkv, w_dkv_s, kv_g, kv_b, w_ukv, w_ukv_s, out_q, out_kv
):
    nc = tc.nc
    with ExitStack() as ctx:
        keep = ctx.enter_context(tc.tile_pool(name="keep", bufs=1))
        work = ctx.enter_context(tc.tile_pool(name="work", bufs=2))
        psum = ctx.enter_context(tc.psum_pool(name="psum", bufs=2))
        ctx.enter_context(tc.manual_schedule())

        rows = keep.tile([P, 4, LAT], BF16, name="rows")
        nc.vector.memset(rows[:].rearrange("p v n -> p (v n)").bitcast(F32), 0.0)
        wsc = keep.tile([P, 2560], U8, align_bytes=64, name="wsc")
        nc.vector.memset(wsc[:].bitcast(I32), 0)
        ones = keep.tile([P, P], BF16, name="ones")
        nc.vector.memset(ones[:], 1.0)
        for v, vec in enumerate((q_g, q_b, kv_g, kv_b)):
            nc.scalar.dma_start(out=rows[0:1, v, :], in_=vec.rearrange("(o n) -> o n", o=1))
        zero = keep.tile([P, 1], F32, name="zero")
        nc.vector.memset(zero[:], 0.0)
        eps = keep.tile([P, 1], F32, name="eps")
        nc.vector.tensor_scalar(out=eps[:], in0=zero[:], scalar1=EPS, scalar2=None, op0=ALU.add)
        dummy = keep.tile([P, 1], F32, name="dummy")
        nc.scalar.activation(out=dummy[:], in_=eps[:], func=ACT.Abs_reciprocal_sqrt)
        ident = keep.tile([P, P], F32, name="ident")
        make_identity(nc, ident[:])

        sc = keep.tile([P, PASSES, PACK], F32, name="sc")
        nc.sync.dma_start(out=sc[:], in_=normed_scale.rearrange("a b (c p m) -> p (a b c) m", p=P, m=PACK))
        x_bytes = [keep.tile([P, D], U8, name=f"x_bytes{i}") for i in range(B)]

        def load_x(i):
            nc.sync.dma_start(out=x_bytes[i][:], in_=normed_bytes[i])

        dq = keep.tile([P, PASSES, LAT], U32, align_bytes=64, name="dq")
        dkv = keep.tile([P, PASSES, LAT], U32, align_bytes=64, name="dkv")
        uq = keep.tile([P, N_Q], U32, align_bytes=64, name="uq")
        ukv = keep.tile([P, N_KV], U32, align_bytes=64, name="ukv")

        def load_down(tile, w):
            nc.sync.dma_start(out=tile[:].bitcast(I32), in_=w.rearrange("g p n t -> p g (n t)").bitcast(I32))

        def load_up(tile, w, c):
            words = w[0].rearrange("p n t -> p (n t)")
            nc.sync.dma_start(out=tile[:, c:c + 2048].bitcast(I32), in_=words[:, 4 * c:4 * (c + 2048)].bitcast(I32))

        def load_down_scales(col, s):
            for q in range(4):
                nc.sync.dma_start(out=wsc[32 * q:32 * q + 16, col:col + LAT].bitcast(I32), in_=s[:, 4 * q:4 * q + 4, :].bitcast(I32))

        def load_up_scales(col, s, n):
            w = n // 4
            for q in range(4):
                nc.sync.dma_start(out=wsc[32 * q:32 * q + 16, col:col + w].bitcast(I32), in_=s[0, 4 * q:4 * q + 4, :].rearrange("r (j n) -> j r n", j=4).bitcast(I32))

        load_x(0)
        load_x(1)
        load_down_scales(512, w_dkv_s)
        load_down(dkv, w_dkv)
        load_up_scales(1536, w_ukv_s, N_KV)
        load_up(ukv, w_ukv, 0)
        load_x(2)
        load_up(ukv, w_ukv, 2048)
        load_x(3)
        load_down_scales(0, w_dq_s)
        load_up_scales(1024, w_uq_s, N_Q)
        load_down(dq, w_dq)
        load_up(uq, w_uq, 0)

        affine = [keep.tile([P, LAT], F32, name=f"affine{v}") for v in range(4)]

        abank = {}

        def amm(v):
            bank = psum.tile([P, LAT], F32, tag="turn", bufs=NT, name="bank")
            nc.tensor.matmul(bank[:], lhsT=ones[:], rhs=rows[:, v, :], start=True, stop=True)
            abank[v] = bank

        def acopy(v):
            nc.scalar.copy(out=affine[v][:], in_=abank[v][:])

        xbank = {}
        xb, xg, xq, xs = {}, {}, {}, {}

        def cast(i, c):
            if i not in xb:
                xb[i] = work.tile([P, D], BF16, tag="xb", bufs=4, name="xb")
            cols = slice(c * K_PASS, (c + 1) * K_PASS)
            src = x_bytes[i][:, cols].bitcast(FP8)
            if i in GCAST:
                nc.gpsimd.tensor_copy(out=xb[i][:, cols], in_=src)
            elif i == 0 and c % 2 == 1:
                nc.vector.tensor_copy(out=xb[i][:, cols], in_=src)
            else:
                nc.scalar.copy(out=xb[i][:, cols], in_=src)

        def turn(i, h):
            bank = psum.tile([P, 2, 2, P], F32, tag="turn", bufs=NT, name="bank")
            words = xb[i][:].bitcast(F32)
            for g in range(2):
                base = 256 * (2 * h + g)
                for u in range(2):
                    nc.tensor.transpose(bank[:, g, u, :], words[:, base + u:base + 256:2], ident[:])
            xbank[i, h] = bank

        def scale(i, c):
            h, g = divmod(c, 2)
            if i not in xg:
                xg[i] = work.tile([P, PASSES, P, PACK], BF16, tag="xg", bufs=4, align_bytes=64, name="xg")
            nc.vector.tensor_tensor(
                out=xg[i][:, c].rearrange("p r (u e) -> p r u e", e=2),
                in0=xbank[i, h][:, g].bitcast(BF16).rearrange("p u (r e) -> p r u e", e=2),
                in1=sc[:, c, :].rearrange("p (u e) -> p u e", e=2).unsqueeze(1).to_broadcast([P, P, 2, 2]),
                op=ALU.mult,
            )

        def qx(i, h):
            if i not in xq:
                xq[i] = keep.tile([P, PASSES, P], U32, align_bytes=64, name=f"xq{i}")
                xs[i] = keep.tile([P, PASSES, P], U8, align_bytes=64, name=f"xs{i}")
            g = slice(0, PASSES) if h == 2 else slice(2 * h, 2 * h + 2)
            nc.vector.quantize_mx(
                out=xq[i][:, g, :].rearrange("p g r -> p (g r)").bitcast(FP8X4),
                scales=xs[i][:, g, :].rearrange("p g r -> p (g r)"),
                in_=xg[i][:, g].rearrange("p g r t -> p (g r t)"),
            )

        down = {"q": (dq, 0, 0), "kv": (dkv, 512, 2)}
        up = {"q": (uq, 1024, N_Q, out_q), "kv": (ukv, 1536, N_KV, out_kv)}
        half = {"kv": (0, 1), "q": (1, 2), "j": (0, 2)}
        lat, cen, mv, inv, cn, cg, cq, cs, lbank, obank, six = ({} for v in range(11))

        def project(i, path):
            w, col, _ = down[path]
            acc = psum.tile([P, LAT], F32, tag="lat", bufs=NL, name="lat")
            for g in range(PASSES):
                nc.tensor.matmul_mx(
                    out=acc[:],
                    lhsT=xq[i][:, g, :].bitcast(FP8X4),
                    lhsT_scale=xs[i][:, g, :],
                    rhs=w[:, g, :].bitcast(FP8X4),
                    rhs_scale=wsc[4 * g:P, col:col + LAT],
                    start=(g == 0),
                    stop=(g == PASSES - 1),
                )
            lat[i, path] = acc

        def stats(i, path):
            t = work.tile([P, 6], F32, tag="six", bufs=8, name="six")
            nc.vector.bn_stats(out=t[:], in_=lat[i, path][:])
            six[i, path] = t

        def agg(i, path):
            if i not in mv:
                mv[i] = work.tile([P, 2, 2], F32, tag="mv", bufs=4, name="mv")
                inv[i] = work.tile([P, 2], F32, tag="inv", bufs=4, name="inv")
                cn[i] = work.tile([P, 2, LAT], BF16, tag="cn", bufs=4, name="cn")
                cg[i] = work.tile([P, 2, P, PACK], BF16, tag="cg", bufs=4, align_bytes=64, name="cg")
                cq[i] = work.tile([P, 2, P], U32, tag="cq", bufs=4, align_bytes=64, name="cq")
                cs[i] = work.tile([P, 2, P], U8, tag="cs", bufs=4, align_bytes=64, name="cs")
            a, b = half[path]
            nc.vector.bn_aggr(out=mv[i][:, a, :], in_=six[i, path][:])

        def power_of(i, path):
            a, b = half[path]
            nc.scalar.activation(out=inv[i][:, a:b], in_=mv[i][:, a:b, 1], func=ACT.Abs_reciprocal_sqrt, bias=eps[:], scale=1.0)

        def center(i, path):
            a, b = half[path]
            v = down[path][2]
            t = work.tile([P, LAT], F32, tag="cen", bufs=8, name="cen")
            nc.vector.scalar_tensor_tensor(out=t[:], in0=lat[i, path][:], scalar=mv[i][:, a, 0:1], in1=affine[v][:], op0=ALU.subtract, op1=ALU.mult)
            cen[i, path] = t

        def finish(i, path):
            a, b = half[path]
            v = down[path][2]
            nc.vector.scalar_tensor_tensor(out=cn[i][:, a, :], in0=cen[i, path][:], scalar=inv[i][:, a:b], in1=affine[v + 1][:], op0=ALU.mult, op1=ALU.add)

        def tl(i, path):
            a, b = half[path]
            bank = psum.tile([P, 2, 2, P], F32, tag="turn", bufs=NT, name="bank")
            for k in range(a, b):
                words = cn[i][:, k, :].bitcast(F32)
                for u in range(2):
                    nc.tensor.transpose(bank[:, k, u, :], words[:, u:256:2], ident[:])
            lbank[i, path] = bank

        def ll(i, path):
            a, b = half[path]
            nc.scalar.copy(
                out=cg[i][:, a:b].rearrange("p k r t -> p k (r t)").bitcast(F32).rearrange("p k (r u) -> p k r u", u=2),
                in_=lbank[i, path][:, a:b].rearrange("p k u r -> p k r u"),
            )

        def ql(i, path):
            a, b = half[path]
            nc.vector.quantize_mx(
                out=cq[i][:, a:b, :].rearrange("p k r -> p (k r)").bitcast(FP8X4),
                scales=cs[i][:, a:b, :].rearrange("p k r -> p (k r)"),
                in_=cg[i][:, a:b].rearrange("p k r t -> p (k r t)"),
            )

        res = {}

        def mm(i, path, n):
            w, col, width, out = up[path]
            a, b = half[path]
            j, within = divmod(n * BANK, width // 4)
            bank = psum.tile([P, BANK], F32, tag="bank", bufs=NB, name="bank")
            nc.tensor.matmul_mx(
                out=bank[:],
                lhsT=cq[i][:, a, :].bitcast(FP8X4),
                lhsT_scale=cs[i][:, a, :],
                rhs=w[:, n * BANK:(n + 1) * BANK].bitcast(FP8X4),
                rhs_scale=wsc[4 * j:P, col + within:col + within + BANK],
                start=True,
                stop=True,
            )
            obank[i, path, n] = bank

        def drain(i, path, n, engine):
            out = up[path][3]
            four = (i, path, n // GS)
            if four not in res:
                res[four] = [work.tile([P, GS, BANK], F32, tag="res", bufs=28 // GS, name="res"), 0]
            tile = res[four][0]
            dst = tile[:, n % GS, :]
            if engine == "V":
                nc.vector.tensor_copy(out=dst, in_=obank[i, path, n][:])
            else:
                nc.scalar.copy(out=dst, in_=obank[i, path, n][:])
            res[four][1] += 1
            m = n // GS * GS
            if four == LAST:
                nc.sync.dma_start(out=out[i, :, n * BANK:(n + 1) * BANK], in_=dst)
            elif res[four][1] == GS:
                nc.sync.dma_start(out=out[i, :, m * BANK:(m + GS) * BANK], in_=tile[:].rearrange("p h n -> p (h n)"))

        stages = {"cast": cast, "turn": turn, "scale": scale, "qx": qx, "project": project, "stats": stats, "agg": agg, "pow": power_of, "center": center, "finish": finish, "tl": tl, "ll": ll, "ql": ql, "mm": mm, "drain": drain, "amm": amm, "acopy": acopy}
        for name, *args in ORDER:
            stages[name](*args)
